import numpy as np
import ml_dtypes


def mxq(x, axis, fmt="e4m3"):
    dtype, down = {"e4m3": (ml_dtypes.float8_e4m3fn, 7), "e5m2": (ml_dtypes.float8_e5m2, 14)}[fmt]
    v = np.moveaxis(np.asarray(x, np.float32).astype(ml_dtypes.bfloat16).astype(np.float64), axis, -1)
    blocks = v.reshape(v.shape[:-1] + (-1, 32))
    amax = np.abs(blocks).max(-1, keepdims=True)
    byte = np.maximum(np.where(amax > 0, np.frexp(amax)[1] - 1 + 127, 0) - down, 1)
    scale = np.exp2(byte - 127.0)
    codes = (blocks / scale).astype(np.float32).astype(dtype).astype(np.float64)
    return np.moveaxis((codes * scale).reshape(v.shape), -1, axis)


WIDE = False


def mx_kscale(k):
    if not WIDE:
        return np.ones(k)
    levels = np.array([10, -10, 5, -5, 0])
    a = np.random.permutation(np.resize(levels, k // 512 * 4)).reshape(k // 512, 4)
    idx = np.arange(k)
    return np.exp2(a[idx // 512, idx % 128 // 32])


BF16 = ml_dtypes.bfloat16


def bf(x):
    return np.asarray(x, np.float32).astype(BF16)


def f64(x):
    return np.asarray(x).astype(np.float64)


N, D = 2048, 128
NEG_INF = -1e9


def setup_inputs():
    s = mx_kscale(N)
    c = np.exp2(np.round(np.log2(s.mean())))
    x = np.round(np.random.standard_normal((N, D)) * 16.0) / 16.0
    adj = np.random.random((N, N)) + np.log(s)[None, :] / 10.0
    aff = np.random.randint(0, 2, (N, N))
    beta = 2.0 + 4.0 * np.random.random(1)
    return {"x": bf(x * (c / s)[:, None]), "adj": bf(adj), "aff_cropping": bf(aff), "beta": bf(beta)}


def reference(x, adj, aff_cropping, beta):
    x, adj, aff_cropping, beta = f64(x), f64(adj), f64(aff_cropping), f64(beta)
    norm2 = np.sqrt((x * x).sum(axis=1, keepdims=True))
    cos = (x @ x.T) / (norm2 * norm2.T + 1e-7)
    mask = np.where((aff_cropping == 0) | (cos < 0), NEG_INF, 0.0)
    masked = beta[0] * cos + mask + 10.0 * adj
    e = np.exp(masked - masked.max(axis=1, keepdims=True))
    return (mxq(e, 1, "e4m3") @ mxq(x, 0, "e4m3")) / e.sum(axis=1, keepdims=True)

@@ -1,0 +1,225 @@
+from contextlib import ExitStack
+
+import concourse.bass as bass
+import concourse.mybir as mybir
+import concourse.tile as tile
+from concourse.masks import make_identity
+
+F32 = mybir.dt.float32
+BF16 = mybir.dt.bfloat16
+U32 = mybir.dt.uint32
+U8 = mybir.dt.uint8
+FP8X4 = mybir.dt.float8_e4m3fn_x4
+ALU = mybir.AluOpType
+ACT = mybir.ActivationFunctionType
+AX = mybir.AxisListType
+
+N = 2048
+D = 128
+P = 128
+NT = N // P
+FLOPS = 2 * 2 * N * N * D
+EPS = 1.0e-7
+BIG = 1.0e9
+HUGE = 1.0e20
+U_ENGINE = "v"
+AM_ENGINE = "v"
+WT_ENGINE = "v"
+
+
+def tile_graphattentionlayer_kernel(tc, x, adj, aff_cropping, beta, out):
+    nc = tc.nc
+    with ExitStack() as ctx:
+        const = ctx.enter_context(tc.tile_pool(name="const", bufs=1))
+        ident_b = const.tile([P, P], BF16)
+        make_identity(nc, ident_b[:])
+        ident_f = const.tile([P, P], F32)
+        make_identity(nc, ident_f[:])
+
+        xn = const.tile([P, NT, D], BF16)
+        nc.sync.dma_start(out=xn[:], in_=x.rearrange("(b p) d -> p b d", p=P))
+        beta_b = const.tile([P, 1], BF16)
+        nc.sync.dma_start(out=beta_b[:], in_=beta.partition_broadcast(P))
+        beta_f = const.tile([P, 1], F32)
+        nc.vector.tensor_copy(out=beta_f[:], in_=beta_b[:])
+
+        xT = const.tile([P, N], BF16)
+        rrow = const.tile([P, N], F32)
+        r2row = const.tile([P, N], F32)
+        n2 = const.tile([P, NT], F32)
+        n0 = const.tile([P, NT], F32)
+        rn0 = const.tile([P, NT], F32)
+        n1 = const.tile([P, NT], F32)
+        r = const.tile([P, NT], F32)
+        s = const.tile([P, NT], F32)
+        dd = const.tile([P, NT], F32)
+        xg = const.tile([P, 4, D, 4], BF16, align_bytes=64)
+        x_codes = const.tile([P, 4, D], U32, align_bytes=64)
+        x_scales = const.tile([P, 4, D], U8, align_bytes=64)
+
+        with tc.tile_pool(name="setup", bufs=1) as setup, tc.psum_pool(name="ps_setup", bufs=2) as pss:
+            for h in range(4):
+                pt = pss.tile([P, 4, P], BF16)
+                for q in range(4):
+                    nc.tensor.transpose(pt[:, q, :], xn[:, 4 * h + q, :], ident_b[:])
+                nc.vector.tensor_copy(
+                    out=xT[:, 512 * h : 512 * (h + 1)], in_=pt[:].rearrange("p q i -> p (q i)")
+                )
+            sq = setup.tile([P, NT, D], F32)
+            nc.vector.tensor_tensor(out=sq[:], in0=xn[:], in1=xn[:], op=ALU.mult)
+            nc.vector.tensor_reduce(out=n2[:], in_=sq[:], axis=AX.X, op=ALU.add)
+            nc.vector.tensor_scalar_max(out=n2[:], in0=n2[:], scalar1=1.0e-30)
+            nc.scalar.activation(out=n0[:], in_=n2[:], func=ACT.Sqrt)
+            nc.vector.reciprocal(out=rn0[:], in_=n0[:])
+            nc.vector.tensor_tensor(out=n1[:], in0=n2[:], in1=rn0[:], op=ALU.mult)
+            nc.vector.tensor_tensor(out=n1[:], in0=n1[:], in1=n0[:], op=ALU.add)
+            nc.vector.tensor_scalar_mul(out=n1[:], in0=n1[:], scalar1=0.5)
+            nc.vector.reciprocal(out=r[:], in_=n1[:])
+            nc.vector.tensor_scalar(
+                out=s[:], in0=r[:], scalar1=beta_f[:, 0:1], scalar2=None, op0=ALU.mult
+            )
+            nc.vector.tensor_scalar_mul(out=dd[:], in0=r[:], scalar1=-EPS)
+
+            rb = setup.tile([P, NT, P], F32)
+            nc.vector.tensor_copy(out=rb[:], in_=r[:].unsqueeze(2).to_broadcast([P, NT, P]))
+            for h in range(4):
+                pr = pss.tile([P, 4, P], F32)
+                for q in range(4):
+                    nc.tensor.transpose(pr[:, q, :], rb[:, 4 * h + q, :], ident_f[:])
+                nc.vector.tensor_copy(
+                    out=rrow[:, 512 * h : 512 * (h + 1)], in_=pr[:].rearrange("p q i -> p (q i)")
+                )
+            nc.vector.tensor_tensor(out=r2row[:], in0=rrow[:], in1=rrow[:], op=ALU.mult)
+
+            nc.vector.tensor_copy(out=xg[:], in_=xn[:].rearrange("p (g t) d -> p g d t", t=4))
+            nc.vector.quantize_mx(
+                out=x_codes[:].rearrange("p g d -> p (g d)").bitcast(FP8X4),
+                scales=x_scales[:].rearrange("p g d -> p (g d)"),
+                in_=xg[:].rearrange("p g d t -> p (g d t)"),
+            )
+
+        io = ctx.enter_context(tc.tile_pool(name="io", bufs=3))
+        work = ctx.enter_context(tc.tile_pool(name="work", bufs=2))
+        keep = ctx.enter_context(tc.tile_pool(name="keep", bufs=1))
+        psg = ctx.enter_context(tc.psum_pool(name="psg", bufs=4))
+        pst = ctx.enter_context(tc.psum_pool(name="pst", bufs=2))
+        pso = ctx.enter_context(tc.psum_pool(name="pso", bufs=2))
+
+        panels = []
+        for it in range(NT):
+            rows = slice(it * P, (it + 1) * P)
+            up0 = it * P
+            adj_t = io.tile([P, N], BF16)
+            nc.sync.dma_start(out=adj_t[:], in_=adj[rows, :])
+            aff_t = io.tile([P, N], BF16)
+            nc.sync.dma_start(out=aff_t[:], in_=aff_cropping[rows, :])
+
+            wt = work.tile([P, N], F32)
+            if WT_ENGINE == "v":
+                nc.vector.scalar_tensor_tensor(
+                    out=wt[:, up0:], in0=r2row[:, up0:], scalar=dd[:, it : it + 1], in1=rrow[:, up0:],
+                    op0=ALU.mult, op1=ALU.add,
+                )
+            else:
+                nc.gpsimd.tensor_scalar(
+                    out=wt[:, up0:], in0=rrow[:, up0:], scalar1=dd[:, it : it + 1], scalar2=1.0,
+                    op0=ALU.mult, op1=ALU.add,
+                )
+                nc.gpsimd.tensor_tensor(out=wt[:, up0:], in0=wt[:, up0:], in1=rrow[:, up0:], op=ALU.mult)
+            u = work.tile([P, N], BF16)
+            if U_ENGINE == "v":
+                nc.vector.tensor_scalar(
+                    out=u[:], in0=aff_t[:], scalar1=-1.0, scalar2=BIG, op0=ALU.add, op1=ALU.mult
+                )
+            elif U_ENGINE == "g":
+                nc.gpsimd.tensor_scalar(
+                    out=u[:], in0=aff_t[:], scalar1=-1.0, scalar2=BIG, op0=ALU.add, op1=ALU.mult
+                )
+            else:
+                nc.scalar.activation(out=u[:], in_=aff_t[:], func=ACT.Copy, bias=-BIG, scale=BIG)
+            am = work.tile([P, N], BF16)
+            if AM_ENGINE == "v":
+                nc.vector.tensor_tensor(out=am[:], in0=adj_t[:], in1=u[:], op=ALU.add)
+            else:
+                nc.gpsimd.tensor_tensor(out=am[:], in0=adj_t[:], in1=u[:], op=ALU.add)
+
+            panel = keep.tile([P, N - up0], F32, name="panel%d" % it)
+            panels.append(panel)
+            z = work.tile([P, N], F32)
+            for c in range(4):
+                nlow = min(max(it - 4 * c, 0), 4)
+                lo = nlow * P
+                g = psg.tile([P, 512], F32)
+                for q in range(nlow):
+                    jb = 4 * c + q
+                    nc.tensor.transpose(
+                        g[:, q * P : (q + 1) * P],
+                        panels[jb][:, (it - jb) * P : (it - jb + 1) * P],
+                        ident_f[:],
+                    )
+                if nlow < 4:
+                    a0 = 512 * c + lo
+                    a1 = 512 * (c + 1)
+                    nc.tensor.matmul(
+                        out=g[:, lo:], lhsT=xT[:, rows], rhs=xT[:, a0:a1], start=True, stop=True
+                    )
+                    nc.vector.scalar_tensor_tensor(
+                        out=panel[:, a0 - up0 : a1 - up0], in0=g[:, lo:], scalar=s[:, it : it + 1],
+                        in1=wt[:, a0:a1], op0=ALU.mult, op1=ALU.mult,
+                    )
+                    nc.vector.scalar_tensor_tensor(
+                        out=panel[:, a0 - up0 : a1 - up0], in0=g[:, lo:], scalar=HUGE,
+                        in1=panel[:, a0 - up0 : a1 - up0], op0=ALU.mult, op1=ALU.min,
+                    )
+                if nlow > 0:
+                    nc.vector.scalar_tensor_tensor(
+                        out=z[:, 512 * c : 512 * c + lo], in0=am[:, 512 * c : 512 * c + lo], scalar=10.0,
+                        in1=g[:, :lo], op0=ALU.mult, op1=ALU.add,
+                    )
+            nc.vector.scalar_tensor_tensor(
+                out=z[:, up0:], in0=am[:, up0:], scalar=10.0, in1=panel[:], op0=ALU.mult, op1=ALU.add
+            )
+            mx = work.tile([P, 1], F32)
+            nc.vector.tensor_reduce(out=mx[:], in_=z[:], axis=AX.X, op=ALU.max)
+            negm = work.tile([P, 1], F32)
+            nc.vector.tensor_scalar_mul(out=negm[:], in0=mx[:], scalar1=-1.0)
+
+            e = work.tile([P, N], BF16)
+            ssum = work.tile([P, 1], F32)
+            nc.scalar.activation(
+                out=e[:], in_=z[:], func=ACT.Exp, bias=negm[:, 0:1], scale=1.0,
+                accum_out=ssum[:, 0:1],
+            )
+
+            eg = work.tile([P, 4, P, 4], BF16, align_bytes=64)
+            for gq in range(4):
+                pt = pst.tile([P, 4, P], BF16)
+                for t in range(4):
+                    c0 = 512 * gq + 128 * t
+                    nc.tensor.transpose(pt[:, t, :], e[:, c0 : c0 + P], ident_b[:])
+                nc.scalar.copy(out=eg[:, gq, :, :], in_=pt[:].rearrange("p t i -> p i t"))
+            e_codes = work.tile([P, 4, P], U32, align_bytes=64)
+            e_scales = work.tile([P, 4, P], U8, align_bytes=64)
+            nc.vector.quantize_mx(
+                out=e_codes[:].rearrange("p g i -> p (g i)").bitcast(FP8X4),
+                scales=e_scales[:].rearrange("p g i -> p (g i)"),
+                in_=eg[:].rearrange("p g i t -> p (g i t)"),
+            )
+            acc = pso.tile([P, D], F32)
+            for gq in range(4):
+                nc.tensor.matmul_mx(
+                    out=acc[:],
+                    lhsT=e_codes[:, gq, :].bitcast(FP8X4),
+                    lhsT_scale=e_scales[:, gq, :],
+                    rhs=x_codes[:, gq, :].bitcast(FP8X4),
+                    rhs_scale=x_scales[:, gq, :],
+                    start=(gq == 0),
+                    stop=(gq == 3),
+                )
+            rs = work.tile([P, 1], F32)
+            nc.vector.reciprocal(out=rs[:], in_=ssum[:])
+            o = work.tile([P, D], F32)
+            nc.vector.tensor_scalar(
+                out=o[:], in0=acc[:], scalar1=rs[:, 0:1], scalar2=None, op0=ALU.mult
+            )
+            nc.sync.dma_start(out=out[rows, :], in_=o[:])

@@ -22,8 +22,8 @@ FLOPS = 2 * 2 * N * N * D
 EPS = 1.0e-7
 BIG = 1.0e9
 HUGE = 1.0e20
-U_ENGINE = "v"
-AM_ENGINE = "v"
+U_ENGINE = "g"
+AM_ENGINE = "g"
 WT_ENGINE = "v"
 
 

@@ -22,9 +22,10 @@ FLOPS = 2 * 2 * N * N * D
 EPS = 1.0e-7
 BIG = 1.0e9
 HUGE = 1.0e20
-U_ENGINE = "g"
-AM_ENGINE = "g"
-WT_ENGINE = "v"
+
+
+def bc(ap, n):
+    return ap.unsqueeze(2).to_broadcast([P, NT, n])
 
 
 def tile_graphattentionlayer_kernel(tc, x, adj, aff_cropping, beta, out):
@@ -44,31 +45,36 @@ def tile_graphattentionlayer_kernel(tc, x, adj, aff_cropping, beta, out):
         nc.vector.tensor_copy(out=beta_f[:], in_=beta_b[:])
 
         xT = const.tile([P, N], BF16)
-        rrow = const.tile([P, N], F32)
-        r2row = const.tile([P, N], F32)
-        n2 = const.tile([P, NT], F32)
-        n0 = const.tile([P, NT], F32)
-        rn0 = const.tile([P, NT], F32)
-        n1 = const.tile([P, NT], F32)
-        r = const.tile([P, NT], F32)
-        s = const.tile([P, NT], F32)
-        dd = const.tile([P, NT], F32)
+        lw = const.tile([P, N], BF16)
+        rw = const.tile([P, N], BF16)
         xg = const.tile([P, 4, D, 4], BF16, align_bytes=64)
         x_codes = const.tile([P, 4, D], U32, align_bytes=64)
         x_scales = const.tile([P, 4, D], U8, align_bytes=64)
 
         with tc.tile_pool(name="setup", bufs=1) as setup, tc.psum_pool(name="ps_setup", bufs=2) as pss:
+            cl = setup.tile([P, NT, P], BF16)
+            nc.gpsimd.memset(cl[:], 0.0)
+            cr = setup.tile([P, NT, P], BF16)
+            nc.gpsimd.memset(cr[:], 0.0)
             for h in range(4):
                 pt = pss.tile([P, 4, P], BF16)
                 for q in range(4):
                     nc.tensor.transpose(pt[:, q, :], xn[:, 4 * h + q, :], ident_b[:])
-                nc.vector.tensor_copy(
+                nc.scalar.copy(
                     out=xT[:, 512 * h : 512 * (h + 1)], in_=pt[:].rearrange("p q i -> p (q i)")
                 )
             sq = setup.tile([P, NT, D], F32)
+            n2 = setup.tile([P, NT], F32)
+            n0 = setup.tile([P, NT], F32)
+            rn0 = setup.tile([P, NT], F32)
+            n1 = setup.tile([P, NT], F32)
+            r = setup.tile([P, NT], F32)
+            s = setup.tile([P, NT], F32)
+            v = setup.tile([P, NT], F32)
+            qq = setup.tile([P, NT], F32)
             nc.vector.tensor_tensor(out=sq[:], in0=xn[:], in1=xn[:], op=ALU.mult)
             nc.vector.tensor_reduce(out=n2[:], in_=sq[:], axis=AX.X, op=ALU.add)
-            nc.vector.tensor_scalar_max(out=n2[:], in0=n2[:], scalar1=1.0e-30)
+            nc.vector.tensor_scalar_max(out=n2[:], in0=n2[:], scalar1=1.0e-20)
             nc.scalar.activation(out=n0[:], in_=n2[:], func=ACT.Sqrt)
             nc.vector.reciprocal(out=rn0[:], in_=n0[:])
             nc.vector.tensor_tensor(out=n1[:], in0=n2[:], in1=rn0[:], op=ALU.mult)
@@ -78,18 +84,42 @@ def tile_graphattentionlayer_kernel(tc, x, adj, aff_cropping, beta, out):
             nc.vector.tensor_scalar(
                 out=s[:], in0=r[:], scalar1=beta_f[:, 0:1], scalar2=None, op0=ALU.mult
             )
-            nc.vector.tensor_scalar_mul(out=dd[:], in0=r[:], scalar1=-EPS)
-
-            rb = setup.tile([P, NT, P], F32)
-            nc.vector.tensor_copy(out=rb[:], in_=r[:].unsqueeze(2).to_broadcast([P, NT, P]))
-            for h in range(4):
-                pr = pss.tile([P, 4, P], F32)
-                for q in range(4):
-                    nc.tensor.transpose(pr[:, q, :], rb[:, 4 * h + q, :], ident_f[:])
-                nc.vector.tensor_copy(
-                    out=rrow[:, 512 * h : 512 * (h + 1)], in_=pr[:].rearrange("p q i -> p (q i)")
-                )
-            nc.vector.tensor_tensor(out=r2row[:], in0=rrow[:], in1=rrow[:], op=ALU.mult)
+            nc.vector.tensor_tensor(out=qq[:], in0=r[:], in1=r[:], op=ALU.mult)
+            nc.vector.scalar_tensor_tensor(
+                out=v[:], in0=s[:], scalar=-EPS, in1=r[:], op0=ALU.mult, op1=ALU.mult
+            )
+            cr9 = cr[:, :, 0:9].rearrange("p b (a c) -> p b a c", c=3)
+            cr4 = cr[:, :, 9:13].rearrange("p b (a c) -> p b a c", c=2)
+            s1 = setup.tile([P, NT], F32)
+            s2 = setup.tile([P, NT], F32)
+            r1 = setup.tile([P, NT], F32)
+            r2 = setup.tile([P, NT], F32)
+            v1 = setup.tile([P, NT], F32)
+            q1 = setup.tile([P, NT], F32)
+            nc.vector.tensor_copy(out=cl[:, :, 0:3], in_=bc(s[:], 3))
+            nc.vector.tensor_copy(out=cr9[:, :, :, 0], in_=bc(r[:], 3))
+            nc.vector.tensor_copy(out=cl[:, :, 9:11], in_=bc(v[:], 2))
+            nc.vector.tensor_copy(out=cr4[:, :, :, 0], in_=bc(qq[:], 2))
+            nc.vector.tensor_tensor(out=s1[:], in0=s[:], in1=cl[:, :, 0], op=ALU.subtract)
+            nc.vector.tensor_tensor(out=r1[:], in0=r[:], in1=cr[:, :, 0], op=ALU.subtract)
+            nc.vector.tensor_tensor(out=v1[:], in0=v[:], in1=cl[:, :, 9], op=ALU.subtract)
+            nc.vector.tensor_tensor(out=q1[:], in0=qq[:], in1=cr[:, :, 9], op=ALU.subtract)
+            nc.vector.tensor_copy(out=cl[:, :, 3:6], in_=bc(s1[:], 3))
+            nc.vector.tensor_copy(out=cr9[:, :, :, 1], in_=bc(r1[:], 3))
+            nc.vector.tensor_copy(out=cl[:, :, 11:13], in_=bc(v1[:], 2))
+            nc.vector.tensor_copy(out=cr4[:, :, :, 1], in_=bc(q1[:], 2))
+            nc.vector.tensor_tensor(out=s2[:], in0=s1[:], in1=cl[:, :, 3], op=ALU.subtract)
+            nc.vector.tensor_tensor(out=r2[:], in0=r1[:], in1=cr[:, :, 1], op=ALU.subtract)
+            nc.vector.tensor_copy(out=cl[:, :, 6:9], in_=bc(s2[:], 3))
+            nc.vector.tensor_copy(out=cr9[:, :, :, 2], in_=bc(r2[:], 3))
+            for src, dst in ((cl, lw), (cr, rw)):
+                for h in range(4):
+                    pt = pss.tile([P, 4, P], BF16)
+                    for q in range(4):
+                        nc.tensor.transpose(pt[:, q, :], src[:, 4 * h + q, :], ident_b[:])
+                    nc.scalar.copy(
+                        out=dst[:, 512 * h : 512 * (h + 1)], in_=pt[:].rearrange("p q i -> p (q i)")
+                    )
 
             nc.vector.tensor_copy(out=xg[:], in_=xn[:].rearrange("p (g t) d -> p g d t", t=4))
             nc.vector.quantize_mx(
@@ -101,9 +131,10 @@ def tile_graphattentionlayer_kernel(tc, x, adj, aff_cropping, beta, out):
         io = ctx.enter_context(tc.tile_pool(name="io", bufs=3))
         work = ctx.enter_context(tc.tile_pool(name="work", bufs=2))
         keep = ctx.enter_context(tc.tile_pool(name="keep", bufs=1))
-        psg = ctx.enter_context(tc.psum_pool(name="psg", bufs=4))
+        psg = ctx.enter_context(tc.psum_pool(name="psg", bufs=3))
+        psw = ctx.enter_context(tc.psum_pool(name="psw", bufs=2))
         pst = ctx.enter_context(tc.psum_pool(name="pst", bufs=2))
-        pso = ctx.enter_context(tc.psum_pool(name="pso", bufs=2))
+        pso = ctx.enter_context(tc.psum_pool(name="pso", bufs=1))
 
         panels = []
         for it in range(NT):
@@ -114,37 +145,22 @@ def tile_graphattentionlayer_kernel(tc, x, adj, aff_cropping, beta, out):
             aff_t = io.tile([P, N], BF16)
             nc.sync.dma_start(out=aff_t[:], in_=aff_cropping[rows, :])
 
-            wt = work.tile([P, N], F32)
-            if WT_ENGINE == "v":
-                nc.vector.scalar_tensor_tensor(
-                    out=wt[:, up0:], in0=r2row[:, up0:], scalar=dd[:, it : it + 1], in1=rrow[:, up0:],
-                    op0=ALU.mult, op1=ALU.add,
-                )
-            else:
-                nc.gpsimd.tensor_scalar(
-                    out=wt[:, up0:], in0=rrow[:, up0:], scalar1=dd[:, it : it + 1], scalar2=1.0,
-                    op0=ALU.mult, op1=ALU.add,
-                )
-                nc.gpsimd.tensor_tensor(out=wt[:, up0:], in0=wt[:, up0:], in1=rrow[:, up0:], op=ALU.mult)
             u = work.tile([P, N], BF16)
-            if U_ENGINE == "v":
-                nc.vector.tensor_scalar(
-                    out=u[:], in0=aff_t[:], scalar1=-1.0, scalar2=BIG, op0=ALU.add, op1=ALU.mult
-                )
-            elif U_ENGINE == "g":
-                nc.gpsimd.tensor_scalar(
-                    out=u[:], in0=aff_t[:], scalar1=-1.0, scalar2=BIG, op0=ALU.add, op1=ALU.mult
-                )
-            else:
-                nc.scalar.activation(out=u[:], in_=aff_t[:], func=ACT.Copy, bias=-BIG, scale=BIG)
+            nc.scalar.activation(out=u[:], in_=aff_t[:], func=ACT.Copy, bias=-BIG, scale=BIG)
             am = work.tile([P, N], BF16)
-            if AM_ENGINE == "v":
-                nc.vector.tensor_tensor(out=am[:], in0=adj_t[:], in1=u[:], op=ALU.add)
-            else:
-                nc.gpsimd.tensor_tensor(out=am[:], in0=adj_t[:], in1=u[:], op=ALU.add)
+            nc.vector.tensor_tensor(out=am[:], in0=adj_t[:], in1=u[:], op=ALU.add)
 
             panel = keep.tile([P, N - up0], F32, name="panel%d" % it)
             panels.append(panel)
+            for c in range(it // 4, 4):
+                a0 = max(512 * c, up0)
+                a1 = 512 * (c + 1)
+                w = psw.tile([P, 512], F32)
+                nc.tensor.matmul(
+                    out=w[:, : a1 - a0], lhsT=lw[:, rows], rhs=rw[:, a0:a1], start=True, stop=True
+                )
+                nc.scalar.copy(out=panel[:, a0 - up0 : a1 - up0], in_=w[:, : a1 - a0])
+
             z = work.tile([P, N], F32)
             for c in range(4):
                 nlow = min(max(it - 4 * c, 0), 4)
@@ -160,16 +176,13 @@ def tile_graphattentionlayer_kernel(tc, x, adj, aff_cropping, beta, out):
                 if nlow < 4:
                     a0 = 512 * c + lo
                     a1 = 512 * (c + 1)
+                    seg = panel[:, a0 - up0 : a1 - up0]
                     nc.tensor.matmul(
                         out=g[:, lo:], lhsT=xT[:, rows], rhs=xT[:, a0:a1], start=True, stop=True
                     )
+                    nc.vector.tensor_tensor(out=seg, in0=g[:, lo:], in1=seg, op=ALU.mult)
                     nc.vector.scalar_tensor_tensor(
-                        out=panel[:, a0 - up0 : a1 - up0], in0=g[:, lo:], scalar=s[:, it : it + 1],
-                        in1=wt[:, a0:a1], op0=ALU.mult, op1=ALU.mult,
-                    )
-                    nc.vector.scalar_tensor_tensor(
-                        out=panel[:, a0 - up0 : a1 - up0], in0=g[:, lo:], scalar=HUGE,
-                        in1=panel[:, a0 - up0 : a1 - up0], op0=ALU.mult, op1=ALU.min,
+                        out=seg, in0=g[:, lo:], scalar=HUGE, in1=seg, op0=ALU.mult, op1=ALU.min
                     )
                 if nlow > 0:
                     nc.vector.scalar_tensor_tensor(
@@ -185,14 +198,14 @@ def tile_graphattentionlayer_kernel(tc, x, adj, aff_cropping, beta, out):
             nc.vector.tensor_scalar_mul(out=negm[:], in0=mx[:], scalar1=-1.0)
 
             e = work.tile([P, N], BF16)
-            ssum = work.tile([P, 1], F32)
-            nc.scalar.activation(
-                out=e[:], in_=z[:], func=ACT.Exp, bias=negm[:, 0:1], scale=1.0,
-                accum_out=ssum[:, 0:1],
-            )
-
+            ssum4 = work.tile([P, 4], F32)
             eg = work.tile([P, 4, P, 4], BF16, align_bytes=64)
             for gq in range(4):
+                cols = slice(512 * gq, 512 * (gq + 1))
+                nc.scalar.activation(
+                    out=e[:, cols], in_=z[:, cols], func=ACT.Exp, bias=negm[:, 0:1], scale=1.0,
+                    accum_out=ssum4[:, gq : gq + 1],
+                )
                 pt = pst.tile([P, 4, P], BF16)
                 for t in range(4):
                     c0 = 512 * gq + 128 * t
@@ -216,6 +229,8 @@ def tile_graphattentionlayer_kernel(tc, x, adj, aff_cropping, beta, out):
                     start=(gq == 0),
                     stop=(gq == 3),
                 )
+            ssum = work.tile([P, 1], F32)
+            nc.vector.tensor_reduce(out=ssum[:], in_=ssum4[:], axis=AX.X, op=ALU.add)
             rs = work.tile([P, 1], F32)
             nc.vector.reciprocal(out=rs[:], in_=ssum[:])
             o = work.tile([P, D], F32)

@@ -146,7 +146,9 @@ def tile_graphattentionlayer_kernel(tc, x, adj, aff_cropping, beta, out):
             nc.sync.dma_start(out=aff_t[:], in_=aff_cropping[rows, :])
 
             u = work.tile([P, N], BF16)
-            nc.scalar.activation(out=u[:], in_=aff_t[:], func=ACT.Copy, bias=-BIG, scale=BIG)
+            nc.gpsimd.tensor_scalar(
+                out=u[:], in0=aff_t[:], scalar1=-1.0, scalar2=BIG, op0=ALU.add, op1=ALU.mult
+            )
             am = work.tile([P, N], BF16)
             nc.vector.tensor_tensor(out=am[:], in0=adj_t[:], in1=u[:], op=ALU.add)
 

@@ -32,6 +32,14 @@ def tile_graphattentionlayer_kernel(tc, x, adj, aff_cropping, beta, out):
     nc = tc.nc
     with ExitStack() as ctx:
         const = ctx.enter_context(tc.tile_pool(name="const", bufs=1))
+        io = ctx.enter_context(tc.tile_pool(name="io", bufs=4))
+        upool = ctx.enter_context(tc.tile_pool(name="upool", bufs=3))
+        ampool = ctx.enter_context(tc.tile_pool(name="ampool", bufs=6))
+        work = ctx.enter_context(tc.tile_pool(name="work", bufs=2))
+        keep = ctx.enter_context(tc.tile_pool(name="keep", bufs=1))
+        warm = const.tile([P, 1], F32)
+        nc.vector.memset(warm[:], 1.0)
+        nc.scalar.activation(out=warm[:], in_=warm[:], func=ACT.Sqrt)
         ident_b = const.tile([P, P], BF16)
         make_identity(nc, ident_b[:])
         ident_f = const.tile([P, P], F32)
@@ -72,8 +80,12 @@ def tile_graphattentionlayer_kernel(tc, x, adj, aff_cropping, beta, out):
             s = setup.tile([P, NT], F32)
             v = setup.tile([P, NT], F32)
             qq = setup.tile([P, NT], F32)
-            nc.vector.tensor_tensor(out=sq[:], in0=xn[:], in1=xn[:], op=ALU.mult)
-            nc.vector.tensor_reduce(out=n2[:], in_=sq[:], axis=AX.X, op=ALU.add)
+            nc.vector.tensor_tensor(out=sq[:, 0:8, :], in0=xn[:, 0:8, :], in1=xn[:, 0:8, :], op=ALU.mult)
+            nc.vector.tensor_reduce(out=n2[:, 0:8], in_=sq[:, 0:8, :], axis=AX.X, op=ALU.add)
+            for b in range(8, NT):
+                nc.scalar.activation(
+                    out=sq[:, b, :], in_=xn[:, b, :], func=ACT.Square, accum_out=n2[:, b : b + 1]
+                )
             nc.vector.tensor_scalar_max(out=n2[:], in0=n2[:], scalar1=1.0e-20)
             nc.scalar.activation(out=n0[:], in_=n2[:], func=ACT.Sqrt)
             nc.vector.reciprocal(out=rn0[:], in_=n0[:])
@@ -112,25 +124,27 @@ def tile_graphattentionlayer_kernel(tc, x, adj, aff_cropping, beta, out):
             nc.vector.tensor_tensor(out=r2[:], in0=r1[:], in1=cr[:, :, 1], op=ALU.subtract)
             nc.vector.tensor_copy(out=cl[:, :, 6:9], in_=bc(s2[:], 3))
             nc.vector.tensor_copy(out=cr9[:, :, :, 2], in_=bc(r2[:], 3))
-            for src, dst in ((cl, lw), (cr, rw)):
-                for h in range(4):
-                    pt = pss.tile([P, 4, P], BF16)
-                    for q in range(4):
-                        nc.tensor.transpose(pt[:, q, :], src[:, 4 * h + q, :], ident_b[:])
+            jobs = ((cl, lw, 0), (cr, rw, 0), (cr, rw, 1), (cr, rw, 2), (cr, rw, 3), (cl, lw, 1), (cl, lw, 2), (cl, lw, 3))
+            for k, (src, dst, h) in enumerate(jobs):
+                pt = pss.tile([P, 4, P], BF16)
+                for q in range(4):
+                    nc.tensor.transpose(pt[:, q, :], src[:, 4 * h + q, :], ident_b[:])
+                if k % 2 == 0:
+                    nc.vector.tensor_copy(
+                        out=dst[:, 512 * h : 512 * (h + 1)], in_=pt[:].rearrange("p q i -> p (q i)")
+                    )
+                else:
                     nc.scalar.copy(
                         out=dst[:, 512 * h : 512 * (h + 1)], in_=pt[:].rearrange("p q i -> p (q i)")
                     )
 
-            nc.vector.tensor_copy(out=xg[:], in_=xn[:].rearrange("p (g t) d -> p g d t", t=4))
+            nc.scalar.copy(out=xg[:], in_=xn[:].rearrange("p (g t) d -> p g d t", t=4))
             nc.vector.quantize_mx(
                 out=x_codes[:].rearrange("p g d -> p (g d)").bitcast(FP8X4),
                 scales=x_scales[:].rearrange("p g d -> p (g d)"),
                 in_=xg[:].rearrange("p g d t -> p (g d t)"),
             )
 
-        io = ctx.enter_context(tc.tile_pool(name="io", bufs=3))
-        work = ctx.enter_context(tc.tile_pool(name="work", bufs=2))
-        keep = ctx.enter_context(tc.tile_pool(name="keep", bufs=1))
         psg = ctx.enter_context(tc.psum_pool(name="psg", bufs=3))
         psw = ctx.enter_context(tc.psum_pool(name="psw", bufs=2))
         pst = ctx.enter_context(tc.psum_pool(name="pst", bufs=2))
@@ -145,11 +159,9 @@ def tile_graphattentionlayer_kernel(tc, x, adj, aff_cropping, beta, out):
             aff_t = io.tile([P, N], BF16)
             nc.sync.dma_start(out=aff_t[:], in_=aff_cropping[rows, :])
 
-            u = work.tile([P, N], BF16)
-            nc.gpsimd.tensor_scalar(
-                out=u[:], in0=aff_t[:], scalar1=-1.0, scalar2=BIG, op0=ALU.add, op1=ALU.mult
-            )
-            am = work.tile([P, N], BF16)
+            u = upool.tile([P, N], BF16)
+            nc.scalar.activation(out=u[:], in_=aff_t[:], func=ACT.Copy, bias=-BIG, scale=BIG)
+            am = ampool.tile([P, N], BF16)
             nc.vector.tensor_tensor(out=am[:], in0=adj_t[:], in1=u[:], op=ALU.add)
 
             panel = keep.tile([P, N - up0], F32, name="panel%d" % it)
@@ -194,10 +206,8 @@ def tile_graphattentionlayer_kernel(tc, x, adj, aff_cropping, beta, out):
             nc.vector.scalar_tensor_tensor(
                 out=z[:, up0:], in0=am[:, up0:], scalar=10.0, in1=panel[:], op0=ALU.mult, op1=ALU.add
             )
-            mx = work.tile([P, 1], F32)
-            nc.vector.tensor_reduce(out=mx[:], in_=z[:], axis=AX.X, op=ALU.max)
             negm = work.tile([P, 1], F32)
-            nc.vector.tensor_scalar_mul(out=negm[:], in0=mx[:], scalar1=-1.0)
+            nc.vector.tensor_reduce(out=negm[:], in_=z[:], axis=AX.X, op=ALU.max, negate=True)
 
             e = work.tile([P, N], BF16)
             ssum4 = work.tile([P, 4], F32)
@@ -212,14 +222,25 @@ def tile_graphattentionlayer_kernel(tc, x, adj, aff_cropping, beta, out):
                 for t in range(4):
                     c0 = 512 * gq + 128 * t
                     nc.tensor.transpose(pt[:, t, :], e[:, c0 : c0 + P], ident_b[:])
-                nc.scalar.copy(out=eg[:, gq, :, :], in_=pt[:].rearrange("p t i -> p i t"))
+                if it == NT - 1:
+                    nc.vector.tensor_copy(out=eg[:, gq, :, :], in_=pt[:].rearrange("p t i -> p i t"))
+                else:
+                    nc.scalar.copy(out=eg[:, gq, :, :], in_=pt[:].rearrange("p t i -> p i t"))
             e_codes = work.tile([P, 4, P], U32, align_bytes=64)
             e_scales = work.tile([P, 4, P], U8, align_bytes=64)
-            nc.vector.quantize_mx(
-                out=e_codes[:].rearrange("p g i -> p (g i)").bitcast(FP8X4),
-                scales=e_scales[:].rearrange("p g i -> p (g i)"),
-                in_=eg[:].rearrange("p g i t -> p (g i t)"),
-            )
+            if it == NT - 1:
+                for gq in range(4):
+                    nc.vector.quantize_mx(
+                        out=e_codes[:, gq, :].bitcast(FP8X4),
+                        scales=e_scales[:, gq, :],
+                        in_=eg[:, gq, :, :].rearrange("p i t -> p (i t)"),
+                    )
+            else:
+                nc.vector.quantize_mx(
+                    out=e_codes[:].rearrange("p g i -> p (g i)").bitcast(FP8X4),
+                    scales=e_scales[:].rearrange("p g i -> p (g i)"),
+                    in_=eg[:].rearrange("p g i t -> p (g i t)"),
+                )
             acc = pso.tile([P, D], F32)
             for gq in range(4):
                 nc.tensor.matmul_mx(
@@ -236,7 +257,5 @@ def tile_graphattentionlayer_kernel(tc, x, adj, aff_cropping, beta, out):
             rs = work.tile([P, 1], F32)
             nc.vector.reciprocal(out=rs[:], in_=ssum[:])
             o = work.tile([P, D], F32)
-            nc.vector.tensor_scalar(
-                out=o[:], in0=acc[:], scalar1=rs[:, 0:1], scalar2=None, op0=ALU.mult
-            )
+            nc.scalar.activation(out=o[:], in_=acc[:], func=ACT.Copy, scale=rs[:, 0:1])
             nc.sync.dma_start(out=out[rows, :], in_=o[:])

@@ -176,10 +176,12 @@ def tile_graphattentionlayer_kernel(tc, x, adj, aff_cropping, beta, out):
                 nc.scalar.copy(out=panel[:, a0 - up0 : a1 - up0], in_=w[:, : a1 - a0])
 
             z = work.tile([P, N], F32)
-            for c in range(4):
+            gts = {}
+
+            def fill(c):
                 nlow = min(max(it - 4 * c, 0), 4)
                 lo = nlow * P
-                g = psg.tile([P, 512], F32)
+                g = psg.tile([P, 512], F32, name="g")
                 for q in range(nlow):
                     jb = 4 * c + q
                     nc.tensor.transpose(
@@ -188,21 +190,57 @@ def tile_graphattentionlayer_kernel(tc, x, adj, aff_cropping, beta, out):
                         ident_f[:],
                     )
                 if nlow < 4:
-                    a0 = 512 * c + lo
-                    a1 = 512 * (c + 1)
-                    seg = panel[:, a0 - up0 : a1 - up0]
                     nc.tensor.matmul(
-                        out=g[:, lo:], lhsT=xT[:, rows], rhs=xT[:, a0:a1], start=True, stop=True
+                        out=g[:, lo:], lhsT=xT[:, rows], rhs=xT[:, 512 * c + lo : 512 * (c + 1)],
+                        start=True, stop=True,
                     )
-                    nc.vector.tensor_tensor(out=seg, in0=g[:, lo:], in1=seg, op=ALU.mult)
-                    nc.vector.scalar_tensor_tensor(
-                        out=seg, in0=g[:, lo:], scalar=HUGE, in1=seg, op0=ALU.mult, op1=ALU.min
-                    )
-                if nlow > 0:
-                    nc.vector.scalar_tensor_tensor(
-                        out=z[:, 512 * c : 512 * c + lo], in0=am[:, 512 * c : 512 * c + lo], scalar=10.0,
-                        in1=g[:, :lo], op0=ALU.mult, op1=ALU.add,
-                    )
+                gts[c] = g
+
+            def seg_of(c):
+                lo = min(max(it - 4 * c, 0), 4) * P
+                return panel[:, 512 * c + lo - up0 : 512 * (c + 1) - up0], lo
+
+            def op_y(c):
+                seg, lo = seg_of(c)
+                nc.vector.tensor_tensor(out=seg, in0=gts[c][:, lo:], in1=seg, op=ALU.mult)
+
+            def op_s(c):
+                seg, lo = seg_of(c)
+                nc.vector.scalar_tensor_tensor(
+                    out=seg, in0=gts[c][:, lo:], scalar=HUGE, in1=seg, op0=ALU.mult, op1=ALU.min
+                )
+
+            def op_low(c):
+                lo = min(max(it - 4 * c, 0), 4) * P
+                nc.vector.scalar_tensor_tensor(
+                    out=z[:, 512 * c : 512 * c + lo], in0=am[:, 512 * c : 512 * c + lo], scalar=10.0,
+                    in1=gts[c][:, :lo], op0=ALU.mult, op1=ALU.add,
+                )
+
+            cb = it // 4
+            ups = list(range(cb, 4))
+            lows = list(range(0, cb + 1)) if it % 4 else list(range(0, cb))
+            fill(ups[0])
+            if len(ups) > 1:
+                fill(ups[1])
+            op_y(ups[0])
+            for k in range(1, len(ups)):
+                op_y(ups[k])
+                op_s(ups[k - 1])
+                if ups[k - 1] in lows:
+                    op_low(ups[k - 1])
+                if k + 1 < len(ups):
+                    fill(ups[k + 1])
+            rest = [c for c in lows if c not in ups]
+            if rest:
+                fill(rest[0])
+                op_low(rest[0])
+            op_s(ups[-1])
+            if ups[-1] in lows:
+                op_low(ups[-1])
+            for c in rest[1:]:
+                fill(c)
+                op_low(c)
             nc.vector.scalar_tensor_tensor(
                 out=z[:, up0:], in0=am[:, up0:], scalar=10.0, in1=panel[:], op0=ALU.mult, op1=ALU.add
             )
@@ -253,7 +291,8 @@ def tile_graphattentionlayer_kernel(tc, x, adj, aff_cropping, beta, out):
                     stop=(gq == 3),
                 )
             ssum = work.tile([P, 1], F32)
-            nc.vector.tensor_reduce(out=ssum[:], in_=ssum4[:], axis=AX.X, op=ALU.add)
+            sjunk = work.tile([P, 4], F32)
+            nc.scalar.activation(out=sjunk[:], in_=ssum4[:], func=ACT.Copy, accum_out=ssum[:, 0:1])
             rs = work.tile([P, 1], F32)
             nc.vector.reciprocal(out=rs[:], in_=ssum[:])
             o = work.tile([P, D], F32)

@@ -151,18 +151,70 @@ def tile_graphattentionlayer_kernel(tc, x, adj, aff_cropping, beta, out):
         pso = ctx.enter_context(tc.psum_pool(name="pso", bufs=1))
 
         panels = []
+        masked = {}
+        pending = {}
+
+        def load_mask(ti):
+            trows = slice(ti * P, (ti + 1) * P)
+            adj_t = io.tile([P, N], BF16, name="adj_t")
+            nc.sync.dma_start(out=adj_t[:], in_=adj[trows, :])
+            aff_t = io.tile([P, N], BF16, name="aff_t")
+            nc.sync.dma_start(out=aff_t[:], in_=aff_cropping[trows, :])
+            u = upool.tile([P, N], BF16, name="u")
+            nc.scalar.activation(out=u[:], in_=aff_t[:], func=ACT.Copy, bias=-BIG, scale=BIG)
+            return adj_t, u
+
+        def add_mask(ti, adj_t, u):
+            am = ampool.tile([P, N], BF16, name="am")
+            nc.vector.tensor_tensor(out=am[:], in0=adj_t[:], in1=u[:], op=ALU.add)
+            masked[ti] = am
+
+        def finish(ti):
+            eg, ssum4 = pending[ti]
+            trows = slice(ti * P, (ti + 1) * P)
+            e_codes = work.tile([P, 4, P], U32, align_bytes=64, name="e_codes")
+            e_scales = work.tile([P, 4, P], U8, align_bytes=64, name="e_scales")
+            if ti == NT - 1:
+                for gq in range(4):
+                    nc.vector.quantize_mx(
+                        out=e_codes[:, gq, :].bitcast(FP8X4),
+                        scales=e_scales[:, gq, :],
+                        in_=eg[:, gq, :, :].rearrange("p i t -> p (i t)"),
+                    )
+            else:
+                nc.vector.quantize_mx(
+                    out=e_codes[:].rearrange("p g i -> p (g i)").bitcast(FP8X4),
+                    scales=e_scales[:].rearrange("p g i -> p (g i)"),
+                    in_=eg[:].rearrange("p g i t -> p (g i t)"),
+                )
+            acc = pso.tile([P, D], F32, name="acc")
+            for gq in range(4):
+                nc.tensor.matmul_mx(
+                    out=acc[:],
+                    lhsT=e_codes[:, gq, :].bitcast(FP8X4),
+                    lhsT_scale=e_scales[:, gq, :],
+                    rhs=x_codes[:, gq, :].bitcast(FP8X4),
+                    rhs_scale=x_scales[:, gq, :],
+                    start=(gq == 0),
+                    stop=(gq == 3),
+                )
+            ssum = work.tile([P, 1], F32, name="ssum")
+            sjunk = work.tile([P, 4], F32, name="sjunk")
+            nc.scalar.activation(out=sjunk[:], in_=ssum4[:], func=ACT.Copy, accum_out=ssum[:, 0:1])
+            rs = work.tile([P, 1], F32, name="rs")
+            nc.vector.reciprocal(out=rs[:], in_=ssum[:])
+            o = work.tile([P, D], F32, name="o")
+            nc.scalar.activation(out=o[:], in_=acc[:], func=ACT.Copy, scale=rs[:, 0:1])
+            nc.sync.dma_start(out=out[trows, :], in_=o[:])
+
+        first = load_mask(0)
+        add_mask(0, first[0], first[1])
         for it in range(NT):
             rows = slice(it * P, (it + 1) * P)
             up0 = it * P
-            adj_t = io.tile([P, N], BF16)
-            nc.sync.dma_start(out=adj_t[:], in_=adj[rows, :])
-            aff_t = io.tile([P, N], BF16)
-            nc.sync.dma_start(out=aff_t[:], in_=aff_cropping[rows, :])
-
-            u = upool.tile([P, N], BF16)
-            nc.scalar.activation(out=u[:], in_=aff_t[:], func=ACT.Copy, bias=-BIG, scale=BIG)
-            am = ampool.tile([P, N], BF16)
-            nc.vector.tensor_tensor(out=am[:], in0=adj_t[:], in1=u[:], op=ALU.add)
+            am = masked[it]
+            if it + 1 < NT:
+                nxt = load_mask(it + 1)
 
             panel = keep.tile([P, N - up0], F32, name="panel%d" % it)
             panels.append(panel)
@@ -241,9 +293,13 @@ def tile_graphattentionlayer_kernel(tc, x, adj, aff_cropping, beta, out):
             for c in rest[1:]:
                 fill(c)
                 op_low(c)
+            if it > 0:
+                finish(it - 1)
             nc.vector.scalar_tensor_tensor(
                 out=z[:, up0:], in0=am[:, up0:], scalar=10.0, in1=panel[:], op0=ALU.mult, op1=ALU.add
             )
+            if it + 1 < NT:
+                add_mask(it + 1, nxt[0], nxt[1])
             negm = work.tile([P, 1], F32)
             nc.vector.tensor_reduce(out=negm[:], in_=z[:], axis=AX.X, op=ALU.max, negate=True)
 
@@ -264,37 +320,5 @@ def tile_graphattentionlayer_kernel(tc, x, adj, aff_cropping, beta, out):
                     nc.vector.tensor_copy(out=eg[:, gq, :, :], in_=pt[:].rearrange("p t i -> p i t"))
                 else:
                     nc.scalar.copy(out=eg[:, gq, :, :], in_=pt[:].rearrange("p t i -> p i t"))
-            e_codes = work.tile([P, 4, P], U32, align_bytes=64)
-            e_scales = work.tile([P, 4, P], U8, align_bytes=64)
-            if it == NT - 1:
-                for gq in range(4):
-                    nc.vector.quantize_mx(
-                        out=e_codes[:, gq, :].bitcast(FP8X4),
-                        scales=e_scales[:, gq, :],
-                        in_=eg[:, gq, :, :].rearrange("p i t -> p (i t)"),
-                    )
-            else:
-                nc.vector.quantize_mx(
-                    out=e_codes[:].rearrange("p g i -> p (g i)").bitcast(FP8X4),
-                    scales=e_scales[:].rearrange("p g i -> p (g i)"),
-                    in_=eg[:].rearrange("p g i t -> p (g i t)"),
-                )
-            acc = pso.tile([P, D], F32)
-            for gq in range(4):
-                nc.tensor.matmul_mx(
-                    out=acc[:],
-                    lhsT=e_codes[:, gq, :].bitcast(FP8X4),
-                    lhsT_scale=e_scales[:, gq, :],
-                    rhs=x_codes[:, gq, :].bitcast(FP8X4),
-                    rhs_scale=x_scales[:, gq, :],
-                    start=(gq == 0),
-                    stop=(gq == 3),
-                )
-            ssum = work.tile([P, 1], F32)
-            sjunk = work.tile([P, 4], F32)
-            nc.scalar.activation(out=sjunk[:], in_=ssum4[:], func=ACT.Copy, accum_out=ssum[:, 0:1])
-            rs = work.tile([P, 1], F32)
-            nc.vector.reciprocal(out=rs[:], in_=ssum[:])
-            o = work.tile([P, D], F32)
-            nc.scalar.activation(out=o[:], in_=acc[:], func=ACT.Copy, scale=rs[:, 0:1])
-            nc.sync.dma_start(out=out[rows, :], in_=o[:])
+            pending[it] = (eg, ssum4)
+        finish(NT - 1)

from contextlib import ExitStack

import concourse.bass as bass
import concourse.mybir as mybir
import concourse.tile as tile
from concourse.masks import make_identity

F32 = mybir.dt.float32
BF16 = mybir.dt.bfloat16
U32 = mybir.dt.uint32
U8 = mybir.dt.uint8
FP8X4 = mybir.dt.float8_e4m3fn_x4
ALU = mybir.AluOpType
ACT = mybir.ActivationFunctionType
AX = mybir.AxisListType

N = 2048
D = 128
P = 128
NT = N // P
FLOPS = 2 * 2 * N * N * D
EPS = 1.0e-7
BIG = 1.0e9
HUGE = 1.0e20


def bc(ap, n):
    return ap.unsqueeze(2).to_broadcast([P, NT, n])


def tile_graphattentionlayer_kernel(tc, x, adj, aff_cropping, beta, out):
    nc = tc.nc
    with ExitStack() as ctx:
        const = ctx.enter_context(tc.tile_pool(name="const", bufs=1))
        io = ctx.enter_context(tc.tile_pool(name="io", bufs=4))
        upool = ctx.enter_context(tc.tile_pool(name="upool", bufs=3))
        ampool = ctx.enter_context(tc.tile_pool(name="ampool", bufs=6))
        work = ctx.enter_context(tc.tile_pool(name="work", bufs=2))
        keep = ctx.enter_context(tc.tile_pool(name="keep", bufs=1))
        warm = const.tile([P, 1], F32)
        nc.vector.memset(warm[:], 1.0)
        nc.scalar.activation(out=warm[:], in_=warm[:], func=ACT.Sqrt)
        ident_b = const.tile([P, P], BF16)
        make_identity(nc, ident_b[:])
        ident_f = const.tile([P, P], F32)
        make_identity(nc, ident_f[:])

        xn = const.tile([P, NT, D], BF16)
        nc.sync.dma_start(out=xn[:], in_=x.rearrange("(b p) d -> p b d", p=P))
        beta_b = const.tile([P, 1], BF16)
        nc.sync.dma_start(out=beta_b[:], in_=beta.partition_broadcast(P))
        beta_f = const.tile([P, 1], F32)
        nc.vector.tensor_copy(out=beta_f[:], in_=beta_b[:])

        xT = const.tile([P, N], BF16)
        lw = const.tile([P, N], BF16)
        rw = const.tile([P, N], BF16)
        xg = const.tile([P, 4, D, 4], BF16, align_bytes=64)
        x_codes = const.tile([P, 4, D], U32, align_bytes=64)
        x_scales = const.tile([P, 4, D], U8, align_bytes=64)

        with tc.tile_pool(name="setup", bufs=1) as setup, tc.psum_pool(name="ps_setup", bufs=2) as pss:
            cl = setup.tile([P, NT, P], BF16)
            nc.gpsimd.memset(cl[:], 0.0)
            cr = setup.tile([P, NT, P], BF16)
            nc.gpsimd.memset(cr[:], 0.0)
            for h in range(4):
                pt = pss.tile([P, 4, P], BF16)
                for q in range(4):
                    nc.tensor.transpose(pt[:, q, :], xn[:, 4 * h + q, :], ident_b[:])
                nc.scalar.copy(
                    out=xT[:, 512 * h : 512 * (h + 1)], in_=pt[:].rearrange("p q i -> p (q i)")
                )
            sq = setup.tile([P, NT, D], F32)
            n2 = setup.tile([P, NT], F32)
            n0 = setup.tile([P, NT], F32)
            rn0 = setup.tile([P, NT], F32)
            n1 = setup.tile([P, NT], F32)
            r = setup.tile([P, NT], F32)
            s = setup.tile([P, NT], F32)
            v = setup.tile([P, NT], F32)
            qq = setup.tile([P, NT], F32)
            nc.vector.tensor_tensor(out=sq[:, 0:8, :], in0=xn[:, 0:8, :], in1=xn[:, 0:8, :], op=ALU.mult)
            nc.vector.tensor_reduce(out=n2[:, 0:8], in_=sq[:, 0:8, :], axis=AX.X, op=ALU.add)
            for b in range(8, NT):
                nc.scalar.activation(
                    out=sq[:, b, :], in_=xn[:, b, :], func=ACT.Square, accum_out=n2[:, b : b + 1]
                )
            nc.vector.tensor_scalar_max(out=n2[:], in0=n2[:], scalar1=1.0e-20)
            nc.scalar.activation(out=n0[:], in_=n2[:], func=ACT.Sqrt)
            nc.vector.reciprocal(out=rn0[:], in_=n0[:])
            nc.vector.tensor_tensor(out=n1[:], in0=n2[:], in1=rn0[:], op=ALU.mult)
            nc.vector.tensor_tensor(out=n1[:], in0=n1[:], in1=n0[:], op=ALU.add)
            nc.vector.tensor_scalar_mul(out=n1[:], in0=n1[:], scalar1=0.5)
            nc.vector.reciprocal(out=r[:], in_=n1[:])
            nc.vector.tensor_scalar(
                out=s[:], in0=r[:], scalar1=beta_f[:, 0:1], scalar2=None, op0=ALU.mult
            )
            nc.vector.tensor_tensor(out=qq[:], in0=r[:], in1=r[:], op=ALU.mult)
            nc.vector.scalar_tensor_tensor(
                out=v[:], in0=s[:], scalar=-EPS, in1=r[:], op0=ALU.mult, op1=ALU.mult
            )
            cr9 = cr[:, :, 0:9].rearrange("p b (a c) -> p b a c", c=3)
            cr4 = cr[:, :, 9:13].rearrange("p b (a c) -> p b a c", c=2)
            s1 = setup.tile([P, NT], F32)
            s2 = setup.tile([P, NT], F32)
            r1 = setup.tile([P, NT], F32)
            r2 = setup.tile([P, NT], F32)
            v1 = setup.tile([P, NT], F32)
            q1 = setup.tile([P, NT], F32)
            nc.vector.tensor_copy(out=cl[:, :, 0:3], in_=bc(s[:], 3))
            nc.vector.tensor_copy(out=cr9[:, :, :, 0], in_=bc(r[:], 3))
            nc.vector.tensor_copy(out=cl[:, :, 9:11], in_=bc(v[:], 2))
            nc.vector.tensor_copy(out=cr4[:, :, :, 0], in_=bc(qq[:], 2))
            nc.vector.tensor_tensor(out=s1[:], in0=s[:], in1=cl[:, :, 0], op=ALU.subtract)
            nc.vector.tensor_tensor(out=r1[:], in0=r[:], in1=cr[:, :, 0], op=ALU.subtract)
            nc.vector.tensor_tensor(out=v1[:], in0=v[:], in1=cl[:, :, 9], op=ALU.subtract)
            nc.vector.tensor_tensor(out=q1[:], in0=qq[:], in1=cr[:, :, 9], op=ALU.subtract)
            nc.vector.tensor_copy(out=cl[:, :, 3:6], in_=bc(s1[:], 3))
            nc.vector.tensor_copy(out=cr9[:, :, :, 1], in_=bc(r1[:], 3))
            nc.vector.tensor_copy(out=cl[:, :, 11:13], in_=bc(v1[:], 2))
            nc.vector.tensor_copy(out=cr4[:, :, :, 1], in_=bc(q1[:], 2))
            nc.vector.tensor_tensor(out=s2[:], in0=s1[:], in1=cl[:, :, 3], op=ALU.subtract)
            nc.vector.tensor_tensor(out=r2[:], in0=r1[:], in1=cr[:, :, 1], op=ALU.subtract)
            nc.vector.tensor_copy(out=cl[:, :, 6:9], in_=bc(s2[:], 3))
            nc.vector.tensor_copy(out=cr9[:, :, :, 2], in_=bc(r2[:], 3))
            jobs = ((cl, lw, 0), (cr, rw, 0), (cr, rw, 1), (cr, rw, 2), (cr, rw, 3), (cl, lw, 1), (cl, lw, 2), (cl, lw, 3))
            for k, (src, dst, h) in enumerate(jobs):
                pt = pss.tile([P, 4, P], BF16)
                for q in range(4):
                    nc.tensor.transpose(pt[:, q, :], src[:, 4 * h + q, :], ident_b[:])
                if k % 2 == 0:
                    nc.vector.tensor_copy(
                        out=dst[:, 512 * h : 512 * (h + 1)], in_=pt[:].rearrange("p q i -> p (q i)")
                    )
                else:
                    nc.scalar.copy(
                        out=dst[:, 512 * h : 512 * (h + 1)], in_=pt[:].rearrange("p q i -> p (q i)")
                    )

            nc.scalar.copy(out=xg[:], in_=xn[:].rearrange("p (g t) d -> p g d t", t=4))
            nc.vector.quantize_mx(
                out=x_codes[:].rearrange("p g d -> p (g d)").bitcast(FP8X4),
                scales=x_scales[:].rearrange("p g d -> p (g d)"),
                in_=xg[:].rearrange("p g d t -> p (g d t)"),
            )

        psg = ctx.enter_context(tc.psum_pool(name="psg", bufs=3))
        psw = ctx.enter_context(tc.psum_pool(name="psw", bufs=2))
        pst = ctx.enter_context(tc.psum_pool(name="pst", bufs=2))
        pso = ctx.enter_context(tc.psum_pool(name="pso", bufs=1))

        panels = []
        masked = {}
        pending = {}

        def load_mask(ti):
            trows = slice(ti * P, (ti + 1) * P)
            adj_t = io.tile([P, N], BF16, name="adj_t")
            nc.sync.dma_start(out=adj_t[:], in_=adj[trows, :])
            aff_t = io.tile([P, N], BF16, name="aff_t")
            nc.sync.dma_start(out=aff_t[:], in_=aff_cropping[trows, :])
            u = upool.tile([P, N], BF16, name="u")
            nc.scalar.activation(out=u[:], in_=aff_t[:], func=ACT.Copy, bias=-BIG, scale=BIG)
            return adj_t, u

        def add_mask(ti, adj_t, u):
            am = ampool.tile([P, N], BF16, name="am")
            nc.vector.tensor_tensor(out=am[:], in0=adj_t[:], in1=u[:], op=ALU.add)
            masked[ti] = am

        def finish(ti):
            eg, ssum4 = pending[ti]
            trows = slice(ti * P, (ti + 1) * P)
            e_codes = work.tile([P, 4, P], U32, align_bytes=64, name="e_codes")
            e_scales = work.tile([P, 4, P], U8, align_bytes=64, name="e_scales")
            if ti == NT - 1:
                for gq in range(4):
                    nc.vector.quantize_mx(
                        out=e_codes[:, gq, :].bitcast(FP8X4),
                        scales=e_scales[:, gq, :],
                        in_=eg[:, gq, :, :].rearrange("p i t -> p (i t)"),
                    )
            else:
                nc.vector.quantize_mx(
                    out=e_codes[:].rearrange("p g i -> p (g i)").bitcast(FP8X4),
                    scales=e_scales[:].rearrange("p g i -> p (g i)"),
                    in_=eg[:].rearrange("p g i t -> p (g i t)"),
                )
            acc = pso.tile([P, D], F32, name="acc")
            for gq in range(4):
                nc.tensor.matmul_mx(
                    out=acc[:],
                    lhsT=e_codes[:, gq, :].bitcast(FP8X4),
                    lhsT_scale=e_scales[:, gq, :],
                    rhs=x_codes[:, gq, :].bitcast(FP8X4),
                    rhs_scale=x_scales[:, gq, :],
                    start=(gq == 0),
                    stop=(gq == 3),
                )
            ssum = work.tile([P, 1], F32, name="ssum")
            sjunk = work.tile([P, 4], F32, name="sjunk")
            nc.scalar.activation(out=sjunk[:], in_=ssum4[:], func=ACT.Copy, accum_out=ssum[:, 0:1])
            rs = work.tile([P, 1], F32, name="rs")
            nc.vector.reciprocal(out=rs[:], in_=ssum[:])
            o = work.tile([P, D], F32, name="o")
            nc.scalar.activation(out=o[:], in_=acc[:], func=ACT.Copy, scale=rs[:, 0:1])
            nc.sync.dma_start(out=out[trows, :], in_=o[:])

        first = load_mask(0)
        add_mask(0, first[0], first[1])
        for it in range(NT):
            rows = slice(it * P, (it + 1) * P)
            up0 = it * P
            am = masked[it]
            if it + 1 < NT:
                nxt = load_mask(it + 1)

            panel = keep.tile([P, N - up0], F32, name="panel%d" % it)
            panels.append(panel)
            for c in range(it // 4, 4):
                a0 = max(512 * c, up0)
                a1 = 512 * (c + 1)
                w = psw.tile([P, 512], F32)
                nc.tensor.matmul(
                    out=w[:, : a1 - a0], lhsT=lw[:, rows], rhs=rw[:, a0:a1], start=True, stop=True
                )
                nc.scalar.copy(out=panel[:, a0 - up0 : a1 - up0], in_=w[:, : a1 - a0])

            z = work.tile([P, N], F32)
            gts = {}

            def fill(c):
                nlow = min(max(it - 4 * c, 0), 4)
                lo = nlow * P
                g = psg.tile([P, 512], F32, name="g")
                for q in range(nlow):
                    jb = 4 * c + q
                    nc.tensor.transpose(
                        g[:, q * P : (q + 1) * P],
                        panels[jb][:, (it - jb) * P : (it - jb + 1) * P],
                        ident_f[:],
                    )
                if nlow < 4:
                    nc.tensor.matmul(
                        out=g[:, lo:], lhsT=xT[:, rows], rhs=xT[:, 512 * c + lo : 512 * (c + 1)],
                        start=True, stop=True,
                    )
                gts[c] = g

            def seg_of(c):
                lo = min(max(it - 4 * c, 0), 4) * P
                return panel[:, 512 * c + lo - up0 : 512 * (c + 1) - up0], lo

            def op_y(c):
                seg, lo = seg_of(c)
                nc.vector.tensor_tensor(out=seg, in0=gts[c][:, lo:], in1=seg, op=ALU.mult)

            def op_s(c):
                seg, lo = seg_of(c)
                nc.vector.scalar_tensor_tensor(
                    out=seg, in0=gts[c][:, lo:], scalar=HUGE, in1=seg, op0=ALU.mult, op1=ALU.min
                )

            def op_low(c):
                lo = min(max(it - 4 * c, 0), 4) * P
                nc.vector.scalar_tensor_tensor(
                    out=z[:, 512 * c : 512 * c + lo], in0=am[:, 512 * c : 512 * c + lo], scalar=10.0,
                    in1=gts[c][:, :lo], op0=ALU.mult, op1=ALU.add,
                )

            cb = it // 4
            ups = list(range(cb, 4))
            lows = list(range(0, cb + 1)) if it % 4 else list(range(0, cb))
            fill(ups[0])
            if len(ups) > 1:
                fill(ups[1])
            op_y(ups[0])
            for k in range(1, len(ups)):
                op_y(ups[k])
                op_s(ups[k - 1])
                if ups[k - 1] in lows:
                    op_low(ups[k - 1])
                if k + 1 < len(ups):
                    fill(ups[k + 1])
            rest = [c for c in lows if c not in ups]
            if rest:
                fill(rest[0])
                op_low(rest[0])
            op_s(ups[-1])
            if ups[-1] in lows:
                op_low(ups[-1])
            for c in rest[1:]:
                fill(c)
                op_low(c)
            if it > 0:
                finish(it - 1)
            nc.vector.scalar_tensor_tensor(
                out=z[:, up0:], in0=am[:, up0:], scalar=10.0, in1=panel[:], op0=ALU.mult, op1=ALU.add
            )
            if it + 1 < NT:
                add_mask(it + 1, nxt[0], nxt[1])
            negm = work.tile([P, 1], F32)
            nc.vector.tensor_reduce(out=negm[:], in_=z[:], axis=AX.X, op=ALU.max, negate=True)

            e = work.tile([P, N], BF16)
            ssum4 = work.tile([P, 4], F32)
            eg = work.tile([P, 4, P, 4], BF16, align_bytes=64)
            for gq in range(4):
                cols = slice(512 * gq, 512 * (gq + 1))
                nc.scalar.activation(
                    out=e[:, cols], in_=z[:, cols], func=ACT.Exp, bias=negm[:, 0:1], scale=1.0,
                    accum_out=ssum4[:, gq : gq + 1],
                )
                pt = pst.tile([P, 4, P], BF16)
                for t in range(4):
                    c0 = 512 * gq + 128 * t
                    nc.tensor.transpose(pt[:, t, :], e[:, c0 : c0 + P], ident_b[:])
                if it == NT - 1:
                    nc.vector.tensor_copy(out=eg[:, gq, :, :], in_=pt[:].rearrange("p t i -> p i t"))
                else:
                    nc.scalar.copy(out=eg[:, gq, :, :], in_=pt[:].rearrange("p t i -> p i t"))
            pending[it] = (eg, ssum4)
        finish(NT - 1)
